import numpy as np
import ml_dtypes

BF16 = ml_dtypes.bfloat16


def bf(x):
    return np.asarray(x, np.float32).astype(BF16)


def f32(x):
    return np.asarray(x, np.float32)


def f64(x):
    return np.asarray(x).astype(np.float64)


def striped(idx):
    return np.tile(idx.reshape(-1, 16).T, (8, 1))


C, S, N, Q = 256, 256, 128, 128


def sigmoid(v):
    return 1.0 / (1.0 + np.exp(-v))


def setup_inputs():
    return {"base": f32(np.random.standard_normal((C, S))), "hsel": f32(np.random.standard_normal((C, N))), "qv": bf(np.random.standard_normal((Q, N))), "b_r": bf(np.random.standard_normal((Q, C)) / np.sqrt(Q)), "offs": striped(np.random.permutation(S)[:N])}


def reference(base, hsel, qv, b_r, offs):
    idx = offs[:16].T.reshape(-1)
    r = sigmoid(f64(b_r).T @ f64(qv))
    out = f64(base).copy()
    out[:, idx] = r * f64(hsel)
    return out

@@ -1,0 +1,48 @@
+import concourse.mybir as mybir
+
+BF16, F32, U16 = mybir.dt.bfloat16, mybir.dt.float32, mybir.dt.uint16
+MULT = mybir.AluOpType.mult
+SIGMOID = mybir.ActivationFunctionType.Sigmoid
+
+P = 128
+C = 256
+S = 256
+N = 128
+Q = 128
+BLOCKS = C // P
+
+FLOPS = 2 * C * N * Q
+
+
+def tile_agatcellwithmlp_kernel(tc, base, hsel, qv, b_r, offs, out):
+    nc = tc.nc
+    with (
+        tc.tile_pool(name="held", bufs=1) as held,
+        tc.tile_pool(name="blocks", bufs=BLOCKS) as blocks,
+        tc.psum_pool(name="psum", bufs=BLOCKS) as psum,
+    ):
+        queries = held.tile([Q, N], BF16)
+        nc.sync.dma_start(queries[:], qv)
+        generator = held.tile([Q, C], BF16)
+        nc.scalar.dma_start(generator[:], b_r)
+        offsets = held.tile([P, N // 16], U16)
+        nc.sync.dma_start(offsets[:], offs)
+
+        windows, hiddens = [], []
+        for b in range(BLOCKS):
+            channels = slice(b * P, (b + 1) * P)
+            window = blocks.tile([P, S], F32)
+            nc.sync.dma_start(window[:], base[channels, :])
+            hidden = blocks.tile([P, N], F32)
+            nc.scalar.dma_start(hidden[:], hsel[channels, :])
+            windows.append(window)
+            hiddens.append(hidden)
+
+        for b in range(BLOCKS):
+            channels = slice(b * P, (b + 1) * P)
+            logits = psum.tile([P, N], F32)
+            nc.tensor.matmul(logits[:], generator[:, channels], queries[:], start=True, stop=True)
+            gate = blocks.tile([P, N], F32)
+            nc.scalar.activation(gate[:], logits[:], SIGMOID)
+            nc.vector.tensor_tensor(windows[b][:].indirect(offsets[:]), gate[:], hiddens[b][:], MULT)
+            nc.sync.dma_start(out[channels, :], windows[b][:])

@@ -31,10 +31,11 @@ def tile_agatcellwithmlp_kernel(tc, base, hsel, qv, b_r, offs, out):
         windows, hiddens = [], []
         for b in range(BLOCKS):
             channels = slice(b * P, (b + 1) * P)
+            queue = nc.sync if b == 0 else nc.gpsimd
             window = blocks.tile([P, S], F32)
-            nc.sync.dma_start(window[:], base[channels, :])
+            queue.dma_start(window[:], base[channels, :])
             hidden = blocks.tile([P, N], F32)
-            nc.scalar.dma_start(hidden[:], hsel[channels, :])
+            queue.dma_start(hidden[:], hsel[channels, :])
             windows.append(window)
             hiddens.append(hidden)
 

@@ -31,11 +31,10 @@ def tile_agatcellwithmlp_kernel(tc, base, hsel, qv, b_r, offs, out):
         windows, hiddens = [], []
         for b in range(BLOCKS):
             channels = slice(b * P, (b + 1) * P)
-            queue = nc.sync if b == 0 else nc.gpsimd
             window = blocks.tile([P, S], F32)
-            queue.dma_start(window[:], base[channels, :])
+            nc.sync.dma_start(window[:], base[channels, :])
             hidden = blocks.tile([P, N], F32)
-            queue.dma_start(hidden[:], hsel[channels, :])
+            nc.sync.dma_start(hidden[:], hsel[channels, :])
             windows.append(window)
             hiddens.append(hidden)
 

@@ -23,25 +23,26 @@ def tile_agatcellwithmlp_kernel(tc, base, hsel, qv, b_r, offs, out):
     ):
         queries = held.tile([Q, N], BF16)
         nc.sync.dma_start(queries[:], qv)
-        generator = held.tile([Q, C], BF16)
-        nc.scalar.dma_start(generator[:], b_r)
         offsets = held.tile([P, N // 16], U16)
         nc.sync.dma_start(offsets[:], offs)
 
-        windows, hiddens = [], []
+        generators, windows, hiddens = [], [], []
         for b in range(BLOCKS):
             channels = slice(b * P, (b + 1) * P)
+            generator = blocks.tile([Q, P], BF16)
+            nc.scalar.dma_start(generator[:], b_r[:, channels])
             window = blocks.tile([P, S], F32)
             nc.sync.dma_start(window[:], base[channels, :])
             hidden = blocks.tile([P, N], F32)
-            nc.sync.dma_start(hidden[:], hsel[channels, :])
+            nc.scalar.dma_start(hidden[:], hsel[channels, :])
+            generators.append(generator)
             windows.append(window)
             hiddens.append(hidden)
 
         for b in range(BLOCKS):
             channels = slice(b * P, (b + 1) * P)
             logits = psum.tile([P, N], F32)
-            nc.tensor.matmul(logits[:], generator[:, channels], queries[:], start=True, stop=True)
+            nc.tensor.matmul(logits[:], generators[b][:], queries[:], start=True, stop=True)
             gate = blocks.tile([P, N], F32)
             nc.scalar.activation(gate[:], logits[:], SIGMOID)
             nc.vector.tensor_tensor(windows[b][:].indirect(offsets[:]), gate[:], hiddens[b][:], MULT)

@@ -10,6 +10,7 @@ S = 256
 N = 128
 Q = 128
 BLOCKS = C // P
+BURST = 256
 
 FLOPS = 2 * C * N * Q
 
@@ -21,7 +22,7 @@ def tile_agatcellwithmlp_kernel(tc, base, hsel, qv, b_r, offs, out):
         tc.tile_pool(name="blocks", bufs=BLOCKS) as blocks,
         tc.psum_pool(name="psum", bufs=BLOCKS) as psum,
     ):
-        queries = held.tile([Q, N], BF16)
+        queries = held.tile([Q, N], BF16, align_bytes=BURST)
         nc.sync.dma_start(queries[:], qv)
         offsets = held.tile([P, N // 16], U16)
         nc.sync.dma_start(offsets[:], offs)
@@ -29,11 +30,11 @@ def tile_agatcellwithmlp_kernel(tc, base, hsel, qv, b_r, offs, out):
         generators, windows, hiddens = [], [], []
         for b in range(BLOCKS):
             channels = slice(b * P, (b + 1) * P)
-            generator = blocks.tile([Q, P], BF16)
+            generator = blocks.tile([Q, P], BF16, align_bytes=BURST)
             nc.scalar.dma_start(generator[:], b_r[:, channels])
-            window = blocks.tile([P, S], F32)
+            window = blocks.tile([P, S], F32, align_bytes=BURST)
             nc.sync.dma_start(window[:], base[channels, :])
-            hidden = blocks.tile([P, N], F32)
+            hidden = blocks.tile([P, N], F32, align_bytes=BURST)
             nc.scalar.dma_start(hidden[:], hsel[channels, :])
             generators.append(generator)
             windows.append(window)

@@ -17,6 +17,8 @@ FLOPS = 2 * C * N * Q
 
 def tile_agatcellwithmlp_kernel(tc, base, hsel, qv, b_r, offs, out):
     nc = tc.nc
+    base_blocks = base.rearrange("(p b) s -> b p s", b=BLOCKS)
+    out_blocks = out.rearrange("(p b) s -> b p s", b=BLOCKS)
     with (
         tc.tile_pool(name="held", bufs=1) as held,
         tc.tile_pool(name="blocks", bufs=BLOCKS) as blocks,
@@ -24,27 +26,25 @@ def tile_agatcellwithmlp_kernel(tc, base, hsel, qv, b_r, offs, out):
     ):
         queries = held.tile([Q, N], BF16, align_bytes=BURST)
         nc.sync.dma_start(queries[:], qv)
+        generator = held.tile([Q, C], BF16, align_bytes=BURST)
+        nc.scalar.dma_start(generator[:], b_r)
         offsets = held.tile([P, N // 16], U16)
         nc.sync.dma_start(offsets[:], offs)
-
-        generators, windows, hiddens = [], [], []
+        hidden = held.tile([P, BLOCKS * N], F32, align_bytes=BURST)
+        nc.scalar.dma_start(hidden[:], hsel.rearrange("(p b) n -> p (b n)", b=BLOCKS))
+        windows = []
         for b in range(BLOCKS):
-            channels = slice(b * P, (b + 1) * P)
-            generator = blocks.tile([Q, P], BF16, align_bytes=BURST)
-            nc.scalar.dma_start(generator[:], b_r[:, channels])
             window = blocks.tile([P, S], F32, align_bytes=BURST)
-            nc.sync.dma_start(window[:], base[channels, :])
-            hidden = blocks.tile([P, N], F32, align_bytes=BURST)
-            nc.scalar.dma_start(hidden[:], hsel[channels, :])
-            generators.append(generator)
+            nc.sync.dma_start(window[:], base_blocks[b])
             windows.append(window)
-            hiddens.append(hidden)
 
+        generator_blocks = generator[:].rearrange("q (p b) -> q b p", b=BLOCKS)
         for b in range(BLOCKS):
-            channels = slice(b * P, (b + 1) * P)
             logits = psum.tile([P, N], F32)
-            nc.tensor.matmul(logits[:], generators[b][:], queries[:], start=True, stop=True)
+            nc.tensor.matmul(logits[:], generator_blocks[:, b, :], queries[:], start=True, stop=True)
             gate = blocks.tile([P, N], F32)
             nc.scalar.activation(gate[:], logits[:], SIGMOID)
-            nc.vector.tensor_tensor(windows[b][:].indirect(offsets[:]), gate[:], hiddens[b][:], MULT)
-            nc.sync.dma_start(out[channels, :], windows[b][:])
+            nc.vector.tensor_tensor(
+                windows[b][:].indirect(offsets[:]), gate[:], hidden[:, b * N : (b + 1) * N], MULT
+            )
+            nc.sync.dma_start(out_blocks[b], windows[b][:])

@@ -25,9 +25,9 @@ def tile_agatcellwithmlp_kernel(tc, base, hsel, qv, b_r, offs, out):
         tc.psum_pool(name="psum", bufs=BLOCKS) as psum,
     ):
         queries = held.tile([Q, N], BF16, align_bytes=BURST)
-        nc.sync.dma_start(queries[:], qv)
+        nc.scalar.dma_start(queries[:], qv)
         generator = held.tile([Q, C], BF16, align_bytes=BURST)
-        nc.scalar.dma_start(generator[:], b_r)
+        nc.sync.dma_start(generator[:], b_r)
         offsets = held.tile([P, N // 16], U16)
         nc.sync.dma_start(offsets[:], offs)
         hidden = held.tile([P, BLOCKS * N], F32, align_bytes=BURST)

@@ -17,8 +17,8 @@ FLOPS = 2 * C * N * Q
 
 def tile_agatcellwithmlp_kernel(tc, base, hsel, qv, b_r, offs, out):
     nc = tc.nc
-    base_blocks = base.rearrange("(p b) s -> b p s", b=BLOCKS)
-    out_blocks = out.rearrange("(p b) s -> b p s", b=BLOCKS)
+    base_blocks = base.rearrange("(b p) s -> b p s", b=BLOCKS)
+    out_blocks = out.rearrange("(b p) s -> b p s", b=BLOCKS)
     with (
         tc.tile_pool(name="held", bufs=1) as held,
         tc.tile_pool(name="blocks", bufs=BLOCKS) as blocks,
@@ -31,17 +31,18 @@ def tile_agatcellwithmlp_kernel(tc, base, hsel, qv, b_r, offs, out):
         offsets = held.tile([P, N // 16], U16)
         nc.sync.dma_start(offsets[:], offs)
         hidden = held.tile([P, BLOCKS * N], F32, align_bytes=BURST)
-        nc.scalar.dma_start(hidden[:], hsel.rearrange("(p b) n -> p (b n)", b=BLOCKS))
+        nc.scalar.dma_start(
+            hidden[:].rearrange("p (b n) -> p b n", b=BLOCKS), hsel.rearrange("(b p) n -> p b n", b=BLOCKS)
+        )
         windows = []
         for b in range(BLOCKS):
             window = blocks.tile([P, S], F32, align_bytes=BURST)
             nc.sync.dma_start(window[:], base_blocks[b])
             windows.append(window)
 
-        generator_blocks = generator[:].rearrange("q (p b) -> q b p", b=BLOCKS)
         for b in range(BLOCKS):
             logits = psum.tile([P, N], F32)
-            nc.tensor.matmul(logits[:], generator_blocks[:, b, :], queries[:], start=True, stop=True)
+            nc.tensor.matmul(logits[:], generator[:, b * P : (b + 1) * P], queries[:], start=True, stop=True)
             gate = blocks.tile([P, N], F32)
             nc.scalar.activation(gate[:], logits[:], SIGMOID)
             nc.vector.tensor_tensor(

@@ -21,8 +21,8 @@ def tile_agatcellwithmlp_kernel(tc, base, hsel, qv, b_r, offs, out):
     out_blocks = out.rearrange("(b p) s -> b p s", b=BLOCKS)
     with (
         tc.tile_pool(name="held", bufs=1) as held,
-        tc.tile_pool(name="blocks", bufs=BLOCKS) as blocks,
-        tc.psum_pool(name="psum", bufs=BLOCKS) as psum,
+        tc.tile_pool(name="blocks", bufs=3) as blocks,
+        tc.psum_pool(name="psum", bufs=3) as psum,
     ):
         queries = held.tile([Q, N], BF16, align_bytes=BURST)
         nc.scalar.dma_start(queries[:], qv)
@@ -40,12 +40,21 @@ def tile_agatcellwithmlp_kernel(tc, base, hsel, qv, b_r, offs, out):
             nc.sync.dma_start(window[:], base_blocks[b])
             windows.append(window)
 
-        for b in range(BLOCKS):
+        half = N // 2
+        pieces = [(0, 0, half), (1, 0, N), (0, half, half)]
+        for b, start, entries in pieces:
+            stop = start + entries
             logits = psum.tile([P, N], F32)
-            nc.tensor.matmul(logits[:], generator[:, b * P : (b + 1) * P], queries[:], start=True, stop=True)
-            gate = blocks.tile([P, N], F32)
-            nc.scalar.activation(gate[:], logits[:], SIGMOID)
-            nc.vector.tensor_tensor(
-                windows[b][:].indirect(offsets[:]), gate[:], hidden[:, b * N : (b + 1) * N], MULT
+            nc.tensor.matmul(
+                logits[:, :entries], generator[:, b * P : (b + 1) * P], queries[:, start:stop], start=True, stop=True
             )
-            nc.sync.dma_start(out_blocks[b], windows[b][:])
+            gate = blocks.tile([P, N], F32)
+            nc.scalar.activation(gate[:, :entries], logits[:, :entries], SIGMOID)
+            nc.vector.tensor_tensor(
+                windows[b][:].indirect(offsets[:, start // 16 : stop // 16]),
+                gate[:, :entries],
+                hidden[:, b * N + start : b * N + stop],
+                MULT,
+            )
+            if stop == N:
+                nc.sync.dma_start(out_blocks[b], windows[b][:])

import concourse.mybir as mybir

BF16, F32, U16 = mybir.dt.bfloat16, mybir.dt.float32, mybir.dt.uint16
MULT = mybir.AluOpType.mult
SIGMOID = mybir.ActivationFunctionType.Sigmoid

P = 128
C = 256
S = 256
N = 128
Q = 128
BLOCKS = C // P
BURST = 256

FLOPS = 2 * C * N * Q


def tile_agatcellwithmlp_kernel(tc, base, hsel, qv, b_r, offs, out):
    nc = tc.nc
    base_blocks = base.rearrange("(b p) s -> b p s", b=BLOCKS)
    out_blocks = out.rearrange("(b p) s -> b p s", b=BLOCKS)
    with (
        tc.tile_pool(name="held", bufs=1) as held,
        tc.tile_pool(name="blocks", bufs=3) as blocks,
        tc.psum_pool(name="psum", bufs=3) as psum,
    ):
        queries = held.tile([Q, N], BF16, align_bytes=BURST)
        nc.scalar.dma_start(queries[:], qv)
        generator = held.tile([Q, C], BF16, align_bytes=BURST)
        nc.sync.dma_start(generator[:], b_r)
        offsets = held.tile([P, N // 16], U16)
        nc.sync.dma_start(offsets[:], offs)
        hidden = held.tile([P, BLOCKS * N], F32, align_bytes=BURST)
        nc.scalar.dma_start(
            hidden[:].rearrange("p (b n) -> p b n", b=BLOCKS), hsel.rearrange("(b p) n -> p b n", b=BLOCKS)
        )
        windows = []
        for b in range(BLOCKS):
            window = blocks.tile([P, S], F32, align_bytes=BURST)
            nc.sync.dma_start(window[:], base_blocks[b])
            windows.append(window)

        half = N // 2
        pieces = [(0, 0, half), (1, 0, N), (0, half, half)]
        for b, start, entries in pieces:
            stop = start + entries
            logits = psum.tile([P, N], F32)
            nc.tensor.matmul(
                logits[:, :entries], generator[:, b * P : (b + 1) * P], queries[:, start:stop], start=True, stop=True
            )
            gate = blocks.tile([P, N], F32)
            nc.scalar.activation(gate[:, :entries], logits[:, :entries], SIGMOID)
            nc.vector.tensor_tensor(
                windows[b][:].indirect(offsets[:, start // 16 : stop // 16]),
                gate[:, :entries],
                hidden[:, b * N + start : b * N + stop],
                MULT,
            )
            if stop == N:
                nc.sync.dma_start(out_blocks[b], windows[b][:])
